import numpy as np
import ml_dtypes


def mxq(x, axis, fmt="e4m3"):
    dtype, down = {"e4m3": (ml_dtypes.float8_e4m3fn, 7), "e5m2": (ml_dtypes.float8_e5m2, 14)}[fmt]
    v = np.moveaxis(np.asarray(x, np.float32).astype(ml_dtypes.bfloat16).astype(np.float64), axis, -1)
    blocks = v.reshape(v.shape[:-1] + (-1, 32))
    amax = np.abs(blocks).max(-1, keepdims=True)
    byte = np.maximum(np.where(amax > 0, np.frexp(amax)[1] - 1 + 127, 0) - down, 1)
    scale = np.exp2(byte - 127.0)
    codes = (blocks / scale).astype(np.float32).astype(dtype).astype(np.float64)
    return np.moveaxis((codes * scale).reshape(v.shape), -1, axis)


WIDE = False


def mx_kscale(k):
    if not WIDE:
        return np.ones(k)
    levels = np.array([10, -10, 5, -5, 0])
    a = np.random.permutation(np.resize(levels, k // 512 * 4)).reshape(k // 512, 4)
    idx = np.arange(k)
    return np.exp2(a[idx // 512, idx % 128 // 32])


BF16 = ml_dtypes.bfloat16


def bf(x):
    return np.asarray(x, np.float32).astype(BF16)


def f64(x):
    return np.asarray(x).astype(np.float64)


B, CIN, H, W, CP, G = 4, 256, 32, 32, 2048, 2
CG = CP // G
CO = CIN // G
HW = H * W
EPS = 1e-5


def setup_inputs():
    s = mx_kscale(CG)
    return {"y": bf((np.random.standard_normal((B, G, CG, HW)) * 2.5 + 1.0) * s[None, None, :, None]),
            "Wz": bf((np.random.standard_normal((G, CO, CG)) / np.sqrt(CG) + 1.5 / CG) / s),
            "gamma": bf(1.0 + 0.1 * np.random.standard_normal(CIN)),
            "beta": bf(0.1 * np.random.standard_normal(CIN)),
            "x": bf(np.random.standard_normal((B, CIN, H, W)))}


def reference(y, Wz, gamma, beta, x):
    z = mxq(f64(Wz), 2, "e4m3") @ mxq(f64(y), 2, "e4m3")
    zr = z.reshape(B, G, CO * HW)
    mu = zr.mean(-1, keepdims=True)
    var = zr.var(-1, keepdims=True)
    zn = ((zr - mu) * (1.0 / np.sqrt(var + EPS))).reshape(B, CIN, H, W)
    return zn * f64(gamma)[None, :, None, None] + f64(beta)[None, :, None, None] + f64(x)

@@ -1,0 +1,247 @@
+from contextlib import ExitStack
+
+import concourse.mybir as mybir
+from concourse.masks import make_identity
+
+F32 = mybir.dt.float32
+BF16 = mybir.dt.bfloat16
+U32 = mybir.dt.uint32
+U8 = mybir.dt.uint8
+FP8X4 = mybir.dt.float8_e4m3fn_x4
+ALU = mybir.AluOpType
+ACT = mybir.ActivationFunctionType
+
+IMAGES = 4
+GROUPS = 2
+UNITS = IMAGES * GROUPS
+CG = 1024
+CO = 128
+HW = 1024
+EPS = 1e-5
+
+P = 128
+PACK = 4
+K_PASS = P * PACK
+PASSES = CG // K_PASS
+BANK = 512
+HALVES = HW // BANK
+
+VECTOR_COLS = 384
+
+FLOPS = 2 * UNITS * CO * CG * HW
+
+
+def tile_spatialcgnl_pb_t_kernel(tc, y, Wz, gamma, beta, x, out):
+    nc = tc.nc
+    with ExitStack() as stack:
+        stack.enter_context(tc.manual_schedule())
+        consts = stack.enter_context(tc.tile_pool(name="consts", bufs=1))
+        inputs = stack.enter_context(tc.tile_pool(name="inputs", bufs=1))
+        work = stack.enter_context(tc.tile_pool(name="work", bufs=3))
+        small = stack.enter_context(tc.tile_pool(name="small", bufs=4))
+        results = stack.enter_context(tc.tile_pool(name="results", bufs=3))
+
+        w_raw = consts.tile([P, GROUPS * CG], BF16)
+        nc.sync.dma_start(
+            out=w_raw[:].rearrange("o (j k) -> o j k", j=GROUPS), in_=Wz.rearrange("j o k -> o j k")
+        )
+        affine_rows = consts.tile([P, P], BF16)
+        nc.vector.memset(affine_rows[:], 0.0)
+        nc.sync.dma_start(out=affine_rows[0:GROUPS, :], in_=gamma.rearrange("(j o) -> j o", j=GROUPS))
+        nc.sync.dma_start(out=affine_rows[GROUPS : 2 * GROUPS, :], in_=beta.rearrange("(j o) -> j o", j=GROUPS))
+
+        y_raw = {}
+        x_raw = {}
+        for unit in range(UNITS):
+            b, j = divmod(unit, GROUPS)
+            for c in range(PASSES):
+                y_raw[unit, c] = inputs.tile([P, PACK, HW], BF16, name="y_raw_%d_%d" % (unit, c))
+                nc.sync.dma_start(
+                    out=y_raw[unit, c][:],
+                    in_=y[b, j, c * K_PASS : (c + 1) * K_PASS, :].rearrange("(p t) n -> p t n", t=PACK),
+                )
+            x_raw[unit] = inputs.tile([P, HW], BF16, name="x_raw_%d" % unit)
+            nc.sync.dma_start(out=x_raw[unit][:], in_=x[b, j * CO : (j + 1) * CO].rearrange("o h w -> o (h w)"))
+
+        identity = consts.tile([P, P], F32)
+        make_identity(nc, identity[:])
+        minus_average = consts.tile([P, P], F32)
+        nc.vector.memset(minus_average[:], -1.0 / P)
+        eps = consts.tile([P, 1], F32)
+        nc.vector.memset(eps[:], EPS)
+        table_warmer = consts.tile([P, 1], F32)
+        nc.scalar.activation(out=table_warmer[:], in_=eps[:], func=ACT.Sqrt)
+
+        w_codes = consts.tile([P, GROUPS * PASSES * CO], U32, align_bytes=64)
+        w_scales = consts.tile([P, GROUPS * PASSES * CO], U8, align_bytes=64)
+        gamma_beta = consts.tile([P, 2 * GROUPS], F32)
+
+        with tc.psum_pool(name="setup_psum", bufs=1) as setup_psum:
+            w_words = w_raw[:].bitcast(F32).rearrange("o (j c p u) -> o j c u p", j=GROUPS, c=PASSES, u=2)
+            words_of_group = CG // 2
+            w_grouped = consts.tile([P, GROUPS * PASSES * CO * PACK], BF16, align_bytes=64)
+            w_grouped_words = w_grouped[:].bitcast(F32)
+            for j in range(GROUPS):
+                w_t = setup_psum.tile([P, PASSES, 2, CO], F32, name="w_t_%d" % j)
+                for c in range(PASSES):
+                    for u in range(2):
+                        nc.tensor.transpose(w_t[:, c, u, :], w_words[:, j, c, u, :], identity[:])
+                nc.vector.tensor_copy(
+                    out=w_grouped_words[:, j * words_of_group : (j + 1) * words_of_group].rearrange(
+                        "p (c o u) -> p c o u", c=PASSES, u=2
+                    ),
+                    in_=w_t[:].rearrange("p c u o -> p c o u"),
+                )
+            nc.vector.quantize_mx(out=w_codes[:].bitcast(FP8X4), scales=w_scales[:], in_=w_grouped[:])
+
+            affine_rows_f32 = consts.tile([P, P], F32)
+            nc.vector.tensor_copy(out=affine_rows_f32[:], in_=affine_rows[:])
+            affine_t = setup_psum.tile([P, P], F32)
+            nc.tensor.transpose(affine_t[:], affine_rows_f32[:], identity[:])
+            nc.vector.tensor_copy(out=gamma_beta[:], in_=affine_t[:, 0 : 2 * GROUPS])
+
+        z_psum = stack.enter_context(tc.psum_pool(name="z_psum", bufs=3 * HALVES, reuse_waits="tile"))
+        moment_psum = stack.enter_context(tc.psum_pool(name="moment_psum", bufs=2, reuse_waits="tile"))
+
+        vector_cols = slice(0, VECTOR_COLS)
+        scalar_cols = slice(VECTOR_COLS, HW)
+        halves = [slice(h * BANK, (h + 1) * BANK) for h in range(HALVES)]
+
+        grouped = {}
+        z = {}
+        mean_var = {}
+        moments = {}
+        deviation = {}
+        gain = {}
+        shift = {}
+        result = {}
+
+        def regroup(unit, c):
+            rows = y_raw[unit, c]
+            grouped[unit, c] = work.tile([P, HW, PACK], BF16, name="grouped", align_bytes=64)
+            nc.vector.tensor_copy(
+                out=grouped[unit, c][:, vector_cols, :].rearrange("p (n i) t -> p n t i", i=4),
+                in_=rows[:, :, vector_cols].rearrange("p t (n i) -> p n t i", i=4),
+            )
+            nc.scalar.copy(
+                out=grouped[unit, c][:, scalar_cols, :].rearrange("p (n i) t -> p n t i", i=4),
+                in_=rows[:, :, scalar_cols].rearrange("p t (n i) -> p n t i", i=4),
+            )
+
+        def quantise_and_multiply(unit, c):
+            j = unit % GROUPS
+            y_codes = work.tile([P, HW], U32, align_bytes=64)
+            y_scales = work.tile([P, HW], U8, align_bytes=64)
+            nc.vector.quantize_mx(
+                out=y_codes[:].bitcast(FP8X4),
+                scales=y_scales[:],
+                in_=grouped[unit, c][:].rearrange("p n t -> p (n t)"),
+            )
+            if c == 0:
+                z[unit] = [z_psum.tile([P, BANK], F32, name="z_%d" % h, tag="z") for h in range(HALVES)]
+            w_cols = slice((j * PASSES + c) * CO, (j * PASSES + c + 1) * CO)
+            for h in range(HALVES):
+                nc.tensor.matmul_mx(
+                    out=z[unit][h][:],
+                    lhsT=w_codes[:, w_cols].bitcast(FP8X4),
+                    lhsT_scale=w_scales[:, w_cols],
+                    rhs=y_codes[:, halves[h]].bitcast(FP8X4),
+                    rhs_scale=y_scales[:, halves[h]],
+                    start=(c == 0),
+                    stop=(c == PASSES - 1),
+                )
+
+        def partition_moments(unit):
+            bank_stats = small.tile([P, HALVES, 6], F32)
+            for h in range(HALVES):
+                nc.vector.bn_stats(out=bank_stats[:, h, :], in_=z[unit][h][:])
+            mean_var[unit] = small.tile([P, 2], F32, name="mean_var")
+            nc.vector.bn_aggr(out=mean_var[unit][:], in_=bank_stats[:].rearrange("p h s -> p (h s)"))
+            moments[unit] = moment_psum.tile([P, 2], F32, name="moments")
+            nc.tensor.matmul(
+                out=moments[unit][:, 0:1], lhsT=minus_average[:], rhs=mean_var[unit][:, 0:1], start=True, stop=True
+            )
+
+        def unit_deviation(unit):
+            centred = small.tile([P, 1], F32)
+            nc.vector.tensor_tensor(
+                out=centred[:], in0=mean_var[unit][:, 0:1], in1=moments[unit][:, 0:1], op=ALU.add
+            )
+            spread = small.tile([P, 1], F32)
+            nc.vector.scalar_tensor_tensor(
+                out=spread[:],
+                in0=centred[:],
+                scalar=centred[:],
+                in1=mean_var[unit][:, 1:2],
+                op0=ALU.mult,
+                op1=ALU.add,
+            )
+            nc.tensor.matmul(out=moments[unit][:, 1:2], lhsT=minus_average[:], rhs=spread[:], start=True, stop=True)
+            deviation[unit] = small.tile([P, 1], F32, name="deviation")
+            nc.scalar.activation(
+                out=deviation[unit][:], in_=moments[unit][:, 1:2], func=ACT.Sqrt, bias=eps[:], scale=-1.0
+            )
+
+        def gain_and_shift(unit):
+            j = unit % GROUPS
+            inverse = small.tile([P, 1], F32)
+            nc.vector.reciprocal(out=inverse[:], in_=deviation[unit][:])
+            gain[unit] = small.tile([P, 1], F32, name="gain")
+            nc.vector.tensor_mul(out=gain[unit][:], in0=inverse[:], in1=gamma_beta[:, j : j + 1])
+            shift[unit] = small.tile([P, 1], F32, name="shift")
+            nc.vector.scalar_tensor_tensor(
+                out=shift[unit][:],
+                in0=gain[unit][:],
+                scalar=moments[unit][:, 0:1],
+                in1=gamma_beta[:, GROUPS + j : GROUPS + j + 1],
+                op0=ALU.mult,
+                op1=ALU.add,
+            )
+
+        def scale_and_add(unit):
+            result[unit] = results.tile([P, HW], F32, name="result")
+            for h in range(HALVES):
+                nc.vector.scalar_tensor_tensor(
+                    out=result[unit][:, halves[h]],
+                    in0=z[unit][h][:],
+                    scalar=gain[unit][:],
+                    in1=x_raw[unit][:, halves[h]],
+                    op0=ALU.mult,
+                    op1=ALU.add,
+                )
+
+        def shift_and_store(unit):
+            b, j = divmod(unit, GROUPS)
+            out_rows = out[b, j * CO : (j + 1) * CO].rearrange("o h w -> o (h w)")
+            for h in range(HALVES):
+                nc.scalar.activation(
+                    out=result[unit][:, halves[h]],
+                    in_=result[unit][:, halves[h]],
+                    func=ACT.Identity,
+                    bias=shift[unit][:],
+                    scale=1.0,
+                )
+                nc.sync.dma_start(out=out_rows[:, halves[h]], in_=result[unit][:, halves[h]])
+
+        def live(unit):
+            return 0 <= unit < UNITS
+
+        for step in range(UNITS + 3):
+            entering, closing, finishing, leaving = step, step - 1, step - 2, step - 3
+            if live(entering):
+                regroup(entering, 0)
+            if live(leaving):
+                shift_and_store(leaving)
+            if live(finishing):
+                unit_deviation(finishing)
+            if live(closing):
+                quantise_and_multiply(closing, 1)
+            if live(entering):
+                regroup(entering, 1)
+            if live(entering):
+                quantise_and_multiply(entering, 0)
+            if live(closing):
+                partition_moments(closing)
+            if live(finishing):
+                gain_and_shift(finishing)
+                scale_and_add(finishing)

@@ -26,7 +26,7 @@ PASSES = CG // K_PASS
 BANK = 512
 HALVES = HW // BANK
 
-VECTOR_COLS = 384
+VECTOR_COLS = 448
 
 FLOPS = 2 * UNITS * CO * CG * HW
 
@@ -52,7 +52,8 @@ def tile_spatialcgnl_pb_t_kernel(tc, y, Wz, gamma, beta, x, out):
 
         y_raw = {}
         x_raw = {}
-        for unit in range(UNITS):
+
+        def load_y(unit):
             b, j = divmod(unit, GROUPS)
             for c in range(PASSES):
                 y_raw[unit, c] = inputs.tile([P, PACK, HW], BF16, name="y_raw_%d_%d" % (unit, c))
@@ -60,8 +61,17 @@ def tile_spatialcgnl_pb_t_kernel(tc, y, Wz, gamma, beta, x, out):
                     out=y_raw[unit, c][:],
                     in_=y[b, j, c * K_PASS : (c + 1) * K_PASS, :].rearrange("(p t) n -> p t n", t=PACK),
                 )
+
+        def load_x(unit):
+            b, j = divmod(unit, GROUPS)
             x_raw[unit] = inputs.tile([P, HW], BF16, name="x_raw_%d" % unit)
             nc.sync.dma_start(out=x_raw[unit][:], in_=x[b, j * CO : (j + 1) * CO].rearrange("o h w -> o (h w)"))
+
+        load_y(0)
+        for unit in range(1, UNITS):
+            load_y(unit)
+            load_x(unit - 1)
+        load_x(UNITS - 1)
 
         identity = consts.tile([P, P], F32)
         make_identity(nc, identity[:])
@@ -70,7 +80,7 @@ def tile_spatialcgnl_pb_t_kernel(tc, y, Wz, gamma, beta, x, out):
         eps = consts.tile([P, 1], F32)
         nc.vector.memset(eps[:], EPS)
         table_warmer = consts.tile([P, 1], F32)
-        nc.scalar.activation(out=table_warmer[:], in_=eps[:], func=ACT.Sqrt)
+        nc.scalar.activation(out=table_warmer[:], in_=eps[:], func=ACT.Abs_reciprocal_sqrt)
 
         w_codes = consts.tile([P, GROUPS * PASSES * CO], U32, align_bytes=64)
         w_scales = consts.tile([P, GROUPS * PASSES * CO], U8, align_bytes=64)
@@ -111,7 +121,6 @@ def tile_spatialcgnl_pb_t_kernel(tc, y, Wz, gamma, beta, x, out):
         z = {}
         mean_var = {}
         moments = {}
-        deviation = {}
         gain = {}
         shift = {}
         result = {}
@@ -162,40 +171,35 @@ def tile_spatialcgnl_pb_t_kernel(tc, y, Wz, gamma, beta, x, out):
                 out=moments[unit][:, 0:1], lhsT=minus_average[:], rhs=mean_var[unit][:, 0:1], start=True, stop=True
             )
 
-        def unit_deviation(unit):
-            centred = small.tile([P, 1], F32)
-            nc.vector.tensor_tensor(
-                out=centred[:], in0=mean_var[unit][:, 0:1], in1=moments[unit][:, 0:1], op=ALU.add
-            )
-            spread = small.tile([P, 1], F32)
-            nc.vector.scalar_tensor_tensor(
-                out=spread[:],
-                in0=centred[:],
-                scalar=centred[:],
-                in1=mean_var[unit][:, 1:2],
-                op0=ALU.mult,
-                op1=ALU.add,
-            )
-            nc.tensor.matmul(out=moments[unit][:, 1:2], lhsT=minus_average[:], rhs=spread[:], start=True, stop=True)
-            deviation[unit] = small.tile([P, 1], F32, name="deviation")
+        def unit_variance(unit):
+            centred_sq = small.tile([P, 1], F32)
             nc.scalar.activation(
-                out=deviation[unit][:], in_=moments[unit][:, 1:2], func=ACT.Sqrt, bias=eps[:], scale=-1.0
+                out=centred_sq[:], in_=moments[unit][:, 0:1], func=ACT.Square, bias=mean_var[unit][:, 0:1], scale=1.0
+            )
+            nc.tensor.matmul(
+                out=moments[unit][:, 1:2], lhsT=minus_average[:], rhs=mean_var[unit][:, 1:2], start=True, stop=False
+            )
+            nc.tensor.matmul(
+                out=moments[unit][:, 1:2], lhsT=minus_average[:], rhs=centred_sq[:], start=False, stop=True
             )
 
         def gain_and_shift(unit):
             j = unit % GROUPS
             inverse = small.tile([P, 1], F32)
-            nc.vector.reciprocal(out=inverse[:], in_=deviation[unit][:])
+            nc.scalar.activation(
+                out=inverse[:], in_=moments[unit][:, 1:2], func=ACT.Abs_reciprocal_sqrt, bias=eps[:], scale=-1.0
+            )
             gain[unit] = small.tile([P, 1], F32, name="gain")
-            nc.vector.tensor_mul(out=gain[unit][:], in0=inverse[:], in1=gamma_beta[:, j : j + 1])
+            nc.scalar.activation(
+                out=gain[unit][:], in_=gamma_beta[:, j : j + 1], func=ACT.Copy, scale=inverse[:]
+            )
             shift[unit] = small.tile([P, 1], F32, name="shift")
-            nc.vector.scalar_tensor_tensor(
+            nc.scalar.activation(
                 out=shift[unit][:],
-                in0=gain[unit][:],
-                scalar=moments[unit][:, 0:1],
-                in1=gamma_beta[:, GROUPS + j : GROUPS + j + 1],
-                op0=ALU.mult,
-                op1=ALU.add,
+                in_=moments[unit][:, 0:1],
+                func=ACT.Identity,
+                bias=gamma_beta[:, GROUPS + j : GROUPS + j + 1],
+                scale=gain[unit][:],
             )
 
         def scale_and_add(unit):
@@ -230,18 +234,17 @@ def tile_spatialcgnl_pb_t_kernel(tc, y, Wz, gamma, beta, x, out):
             entering, closing, finishing, leaving = step, step - 1, step - 2, step - 3
             if live(entering):
                 regroup(entering, 0)
+            if live(finishing):
+                gain_and_shift(finishing)
             if live(leaving):
                 shift_and_store(leaving)
-            if live(finishing):
-                unit_deviation(finishing)
             if live(closing):
                 quantise_and_multiply(closing, 1)
             if live(entering):
                 regroup(entering, 1)
-            if live(entering):
                 quantise_and_multiply(entering, 0)
             if live(closing):
                 partition_moments(closing)
+                unit_variance(closing)
             if live(finishing):
-                gain_and_shift(finishing)
                 scale_and_add(finishing)

@@ -26,7 +26,7 @@ PASSES = CG // K_PASS
 BANK = 512
 HALVES = HW // BANK
 
-VECTOR_COLS = 448
+VECTOR_COLS = 416
 
 FLOPS = 2 * UNITS * CO * CG * HW
 
@@ -40,7 +40,26 @@ def tile_spatialcgnl_pb_t_kernel(tc, y, Wz, gamma, beta, x, out):
         work = stack.enter_context(tc.tile_pool(name="work", bufs=3))
         small = stack.enter_context(tc.tile_pool(name="small", bufs=4))
         results = stack.enter_context(tc.tile_pool(name="results", bufs=3))
+        z_psum = stack.enter_context(tc.psum_pool(name="z_psum", bufs=3 * HALVES))
+        moment_psum = stack.enter_context(tc.psum_pool(name="moment_psum", bufs=2))
 
+        y_raw = {}
+        x_raw = {}
+
+        def load_y(unit, c):
+            b, j = divmod(unit, GROUPS)
+            y_raw[unit, c] = inputs.tile([P, PACK, HW], BF16, name="y_raw_%d_%d" % (unit, c))
+            nc.sync.dma_start(
+                out=y_raw[unit, c][:],
+                in_=y[b, j, c * K_PASS : (c + 1) * K_PASS, :].rearrange("(p t) n -> p t n", t=PACK),
+            )
+
+        def load_x(unit):
+            b, j = divmod(unit, GROUPS)
+            x_raw[unit] = inputs.tile([P, HW], BF16, name="x_raw_%d" % unit)
+            nc.sync.dma_start(out=x_raw[unit][:], in_=x[b, j * CO : (j + 1) * CO].rearrange("o h w -> o (h w)"))
+
+        load_y(0, 0)
         w_raw = consts.tile([P, GROUPS * CG], BF16)
         nc.sync.dma_start(
             out=w_raw[:].rearrange("o (j k) -> o j k", j=GROUPS), in_=Wz.rearrange("j o k -> o j k")
@@ -49,27 +68,10 @@ def tile_spatialcgnl_pb_t_kernel(tc, y, Wz, gamma, beta, x, out):
         nc.vector.memset(affine_rows[:], 0.0)
         nc.sync.dma_start(out=affine_rows[0:GROUPS, :], in_=gamma.rearrange("(j o) -> j o", j=GROUPS))
         nc.sync.dma_start(out=affine_rows[GROUPS : 2 * GROUPS, :], in_=beta.rearrange("(j o) -> j o", j=GROUPS))
-
-        y_raw = {}
-        x_raw = {}
-
-        def load_y(unit):
-            b, j = divmod(unit, GROUPS)
-            for c in range(PASSES):
-                y_raw[unit, c] = inputs.tile([P, PACK, HW], BF16, name="y_raw_%d_%d" % (unit, c))
-                nc.sync.dma_start(
-                    out=y_raw[unit, c][:],
-                    in_=y[b, j, c * K_PASS : (c + 1) * K_PASS, :].rearrange("(p t) n -> p t n", t=PACK),
-                )
-
-        def load_x(unit):
-            b, j = divmod(unit, GROUPS)
-            x_raw[unit] = inputs.tile([P, HW], BF16, name="x_raw_%d" % unit)
-            nc.sync.dma_start(out=x_raw[unit][:], in_=x[b, j * CO : (j + 1) * CO].rearrange("o h w -> o (h w)"))
-
-        load_y(0)
+        load_y(0, 1)
         for unit in range(1, UNITS):
-            load_y(unit)
+            load_y(unit, 0)
+            load_y(unit, 1)
             load_x(unit - 1)
         load_x(UNITS - 1)
 
@@ -86,32 +88,24 @@ def tile_spatialcgnl_pb_t_kernel(tc, y, Wz, gamma, beta, x, out):
         w_scales = consts.tile([P, GROUPS * PASSES * CO], U8, align_bytes=64)
         gamma_beta = consts.tile([P, 2 * GROUPS], F32)
 
-        with tc.psum_pool(name="setup_psum", bufs=1) as setup_psum:
+        def prepare_weights():
             w_words = w_raw[:].bitcast(F32).rearrange("o (j c p u) -> o j c u p", j=GROUPS, c=PASSES, u=2)
-            words_of_group = CG // 2
             w_grouped = consts.tile([P, GROUPS * PASSES * CO * PACK], BF16, align_bytes=64)
-            w_grouped_words = w_grouped[:].bitcast(F32)
+            w_grouped_words = w_grouped[:].bitcast(F32).rearrange("p (j c o u) -> p j c o u", j=GROUPS, c=PASSES, u=2)
             for j in range(GROUPS):
-                w_t = setup_psum.tile([P, PASSES, 2, CO], F32, name="w_t_%d" % j)
+                w_t = z_psum.tile([P, PASSES, 2, CO], F32, tag="z")
                 for c in range(PASSES):
                     for u in range(2):
                         nc.tensor.transpose(w_t[:, c, u, :], w_words[:, j, c, u, :], identity[:])
-                nc.vector.tensor_copy(
-                    out=w_grouped_words[:, j * words_of_group : (j + 1) * words_of_group].rearrange(
-                        "p (c o u) -> p c o u", c=PASSES, u=2
-                    ),
-                    in_=w_t[:].rearrange("p c u o -> p c o u"),
-                )
+                nc.vector.tensor_copy(out=w_grouped_words[:, j], in_=w_t[:].rearrange("p c u o -> p c o u"))
             nc.vector.quantize_mx(out=w_codes[:].bitcast(FP8X4), scales=w_scales[:], in_=w_grouped[:])
 
+        def prepare_affine():
             affine_rows_f32 = consts.tile([P, P], F32)
             nc.vector.tensor_copy(out=affine_rows_f32[:], in_=affine_rows[:])
-            affine_t = setup_psum.tile([P, P], F32)
+            affine_t = z_psum.tile([P, P], F32, tag="z")
             nc.tensor.transpose(affine_t[:], affine_rows_f32[:], identity[:])
             nc.vector.tensor_copy(out=gamma_beta[:], in_=affine_t[:, 0 : 2 * GROUPS])
-
-        z_psum = stack.enter_context(tc.psum_pool(name="z_psum", bufs=3 * HALVES, reuse_waits="tile"))
-        moment_psum = stack.enter_context(tc.psum_pool(name="moment_psum", bufs=2, reuse_waits="tile"))
 
         vector_cols = slice(0, VECTOR_COLS)
         scalar_cols = slice(VECTOR_COLS, HW)
@@ -190,9 +184,7 @@ def tile_spatialcgnl_pb_t_kernel(tc, y, Wz, gamma, beta, x, out):
                 out=inverse[:], in_=moments[unit][:, 1:2], func=ACT.Abs_reciprocal_sqrt, bias=eps[:], scale=-1.0
             )
             gain[unit] = small.tile([P, 1], F32, name="gain")
-            nc.scalar.activation(
-                out=gain[unit][:], in_=gamma_beta[:, j : j + 1], func=ACT.Copy, scale=inverse[:]
-            )
+            nc.scalar.activation(out=gain[unit][:], in_=gamma_beta[:, j : j + 1], func=ACT.Copy, scale=inverse[:])
             shift[unit] = small.tile([P, 1], F32, name="shift")
             nc.scalar.activation(
                 out=shift[unit][:],
@@ -230,21 +222,26 @@ def tile_spatialcgnl_pb_t_kernel(tc, y, Wz, gamma, beta, x, out):
         def live(unit):
             return 0 <= unit < UNITS
 
-        for step in range(UNITS + 3):
-            entering, closing, finishing, leaving = step, step - 1, step - 2, step - 3
-            if live(entering):
-                regroup(entering, 0)
-            if live(finishing):
-                gain_and_shift(finishing)
-            if live(leaving):
-                shift_and_store(leaving)
-            if live(closing):
-                quantise_and_multiply(closing, 1)
+        regroup(0, 0)
+        prepare_weights()
+        prepare_affine()
+        for step in range(UNITS + 4):
+            entering, multiplied, measured, scaled, leaving = step, step - 1, step - 2, step - 3, step - 4
+            if live(multiplied):
+                quantise_and_multiply(multiplied, 1)
+            if live(scaled):
+                scale_and_add(scaled)
             if live(entering):
                 regroup(entering, 1)
+            if live(measured):
+                unit_variance(measured)
+            if live(leaving):
+                shift_and_store(leaving)
+            if live(entering):
                 quantise_and_multiply(entering, 0)
-            if live(closing):
-                partition_moments(closing)
-                unit_variance(closing)
-            if live(finishing):
-                scale_and_add(finishing)
+            if live(multiplied):
+                partition_moments(multiplied)
+            if live(entering + 1):
+                regroup(entering + 1, 0)
+            if live(measured):
+                gain_and_shift(measured)

@@ -59,7 +59,6 @@ def tile_spatialcgnl_pb_t_kernel(tc, y, Wz, gamma, beta, x, out):
             x_raw[unit] = inputs.tile([P, HW], BF16, name="x_raw_%d" % unit)
             nc.sync.dma_start(out=x_raw[unit][:], in_=x[b, j * CO : (j + 1) * CO].rearrange("o h w -> o (h w)"))
 
-        load_y(0, 0)
         w_raw = consts.tile([P, GROUPS * CG], BF16)
         nc.sync.dma_start(
             out=w_raw[:].rearrange("o (j k) -> o j k", j=GROUPS), in_=Wz.rearrange("j o k -> o j k")
@@ -68,6 +67,7 @@ def tile_spatialcgnl_pb_t_kernel(tc, y, Wz, gamma, beta, x, out):
         nc.vector.memset(affine_rows[:], 0.0)
         nc.sync.dma_start(out=affine_rows[0:GROUPS, :], in_=gamma.rearrange("(j o) -> j o", j=GROUPS))
         nc.sync.dma_start(out=affine_rows[GROUPS : 2 * GROUPS, :], in_=beta.rearrange("(j o) -> j o", j=GROUPS))
+        load_y(0, 0)
         load_y(0, 1)
         for unit in range(1, UNITS):
             load_y(unit, 0)
@@ -222,9 +222,9 @@ def tile_spatialcgnl_pb_t_kernel(tc, y, Wz, gamma, beta, x, out):
         def live(unit):
             return 0 <= unit < UNITS
 
-        regroup(0, 0)
         prepare_weights()
         prepare_affine()
+        regroup(0, 0)
         for step in range(UNITS + 4):
             entering, multiplied, measured, scaled, leaving = step, step - 1, step - 2, step - 3, step - 4
             if live(multiplied):

@@ -26,7 +26,7 @@ PASSES = CG // K_PASS
 BANK = 512
 HALVES = HW // BANK
 
-VECTOR_COLS = 416
+VECTOR_COLS = 352
 
 FLOPS = 2 * UNITS * CO * CG * HW
 
@@ -194,30 +194,28 @@ def tile_spatialcgnl_pb_t_kernel(tc, y, Wz, gamma, beta, x, out):
                 scale=gain[unit][:],
             )
 
-        def scale_and_add(unit):
-            result[unit] = results.tile([P, HW], F32, name="result")
+        def scale_add_shift_store(unit):
+            b, j = divmod(unit, GROUPS)
+            out_rows = out[b, j * CO : (j + 1) * CO].rearrange("o h w -> o (h w)")
             for h in range(HALVES):
+                half = results.tile([P, BANK], F32, name="result_%d" % h)
                 nc.vector.scalar_tensor_tensor(
-                    out=result[unit][:, halves[h]],
+                    out=half[:],
                     in0=z[unit][h][:],
                     scalar=gain[unit][:],
                     in1=x_raw[unit][:, halves[h]],
                     op0=ALU.mult,
                     op1=ALU.add,
                 )
-
-        def shift_and_store(unit):
-            b, j = divmod(unit, GROUPS)
-            out_rows = out[b, j * CO : (j + 1) * CO].rearrange("o h w -> o (h w)")
-            for h in range(HALVES):
-                nc.scalar.activation(
-                    out=result[unit][:, halves[h]],
-                    in_=result[unit][:, halves[h]],
-                    func=ACT.Identity,
-                    bias=shift[unit][:],
-                    scale=1.0,
+                nc.gpsimd.tensor_scalar(
+                    out=half[:],
+                    in0=half[:],
+                    scalar1=1.0,
+                    scalar2=shift[unit][:],
+                    op0=ALU.mult,
+                    op1=ALU.add,
                 )
-                nc.sync.dma_start(out=out_rows[:, halves[h]], in_=result[unit][:, halves[h]])
+                nc.sync.dma_start(out=out_rows[:, halves[h]], in_=half[:])
 
         def live(unit):
             return 0 <= unit < UNITS
@@ -225,23 +223,23 @@ def tile_spatialcgnl_pb_t_kernel(tc, y, Wz, gamma, beta, x, out):
         prepare_weights()
         prepare_affine()
         regroup(0, 0)
-        for step in range(UNITS + 4):
-            entering, multiplied, measured, scaled, leaving = step, step - 1, step - 2, step - 3, step - 4
+        for step in range(UNITS + 3):
+            entering, multiplied, measured, scaled = step, step - 1, step - 2, step - 3
             if live(multiplied):
                 quantise_and_multiply(multiplied, 1)
-            if live(scaled):
-                scale_and_add(scaled)
-            if live(entering):
-                regroup(entering, 1)
             if live(measured):
                 unit_variance(measured)
-            if live(leaving):
-                shift_and_store(leaving)
+            if live(scaled):
+                scale_add_shift_store(scaled)
+                if live(multiplied):
+                    partition_moments(multiplied)
             if live(entering):
-                quantise_and_multiply(entering, 0)
-            if live(multiplied):
+                regroup(entering, 1)
+            if live(multiplied) and not live(scaled):
                 partition_moments(multiplied)
-            if live(entering + 1):
-                regroup(entering + 1, 0)
             if live(measured):
                 gain_and_shift(measured)
+            if live(entering):
+                quantise_and_multiply(entering, 0)
+            if live(entering + 1):
+                regroup(entering + 1, 0)

@@ -26,7 +26,7 @@ PASSES = CG // K_PASS
 BANK = 512
 HALVES = HW // BANK
 
-VECTOR_COLS = 352
+VECTOR_COLS = 368
 
 FLOPS = 2 * UNITS * CO * CG * HW
 
@@ -108,27 +108,35 @@ def tile_spatialcgnl_pb_t_kernel(tc, y, Wz, gamma, beta, x, out):
             nc.vector.tensor_copy(out=gamma_beta[:], in_=affine_t[:, 0 : 2 * GROUPS])
 
         vector_cols = slice(0, VECTOR_COLS)
-        scalar_cols = slice(VECTOR_COLS, HW)
+        scalar_middle = (VECTOR_COLS + HW) // 2
+        scalar_parts = [slice(VECTOR_COLS, scalar_middle), slice(scalar_middle, HW)]
         halves = [slice(h * BANK, (h + 1) * BANK) for h in range(HALVES)]
 
         grouped = {}
         z = {}
+        bank_stats = {}
         mean_var = {}
+        inverse = {}
         moments = {}
         gain = {}
         shift = {}
         result = {}
 
-        def regroup(unit, c):
-            rows = y_raw[unit, c]
+        def interleaved(tile_ap, cols):
+            return tile_ap[:, cols, :].rearrange("p (n i) t -> p n t i", i=4)
+
+        def rows_of(tile_ap, cols):
+            return tile_ap[:, :, cols].rearrange("p t (n i) -> p n t i", i=4)
+
+        def regroup_vector(unit, c):
             grouped[unit, c] = work.tile([P, HW, PACK], BF16, name="grouped", align_bytes=64)
             nc.vector.tensor_copy(
-                out=grouped[unit, c][:, vector_cols, :].rearrange("p (n i) t -> p n t i", i=4),
-                in_=rows[:, :, vector_cols].rearrange("p t (n i) -> p n t i", i=4),
+                out=interleaved(grouped[unit, c], vector_cols), in_=rows_of(y_raw[unit, c], vector_cols)
             )
+
+        def regroup_scalar(unit, c, part):
             nc.scalar.copy(
-                out=grouped[unit, c][:, scalar_cols, :].rearrange("p (n i) t -> p n t i", i=4),
-                in_=rows[:, :, scalar_cols].rearrange("p t (n i) -> p n t i", i=4),
+                out=interleaved(grouped[unit, c], scalar_parts[part]), in_=rows_of(y_raw[unit, c], scalar_parts[part])
             )
 
         def quantise_and_multiply(unit, c):
@@ -155,11 +163,13 @@ def tile_spatialcgnl_pb_t_kernel(tc, y, Wz, gamma, beta, x, out):
                 )
 
         def partition_moments(unit):
-            bank_stats = small.tile([P, HALVES, 6], F32)
+            bank_stats[unit] = small.tile([P, HALVES, 6], F32, name="bank_stats")
             for h in range(HALVES):
-                nc.vector.bn_stats(out=bank_stats[:, h, :], in_=z[unit][h][:])
+                nc.vector.bn_stats(out=bank_stats[unit][:, h, :], in_=z[unit][h][:])
+
+        def unit_mean(unit):
             mean_var[unit] = small.tile([P, 2], F32, name="mean_var")
-            nc.vector.bn_aggr(out=mean_var[unit][:], in_=bank_stats[:].rearrange("p h s -> p (h s)"))
+            nc.vector.bn_aggr(out=mean_var[unit][:], in_=bank_stats[unit][:].rearrange("p h s -> p (h s)"))
             moments[unit] = moment_psum.tile([P, 2], F32, name="moments")
             nc.tensor.matmul(
                 out=moments[unit][:, 0:1], lhsT=minus_average[:], rhs=mean_var[unit][:, 0:1], start=True, stop=True
@@ -177,14 +187,21 @@ def tile_spatialcgnl_pb_t_kernel(tc, y, Wz, gamma, beta, x, out):
                 out=moments[unit][:, 1:2], lhsT=minus_average[:], rhs=centred_sq[:], start=False, stop=True
             )
 
-        def gain_and_shift(unit):
-            j = unit % GROUPS
-            inverse = small.tile([P, 1], F32)
+        def inverse_deviation(unit):
+            inverse[unit] = small.tile([P, 1], F32, name="inverse")
             nc.scalar.activation(
-                out=inverse[:], in_=moments[unit][:, 1:2], func=ACT.Abs_reciprocal_sqrt, bias=eps[:], scale=-1.0
+                out=inverse[unit][:], in_=moments[unit][:, 1:2], func=ACT.Abs_reciprocal_sqrt, bias=eps[:], scale=-1.0
             )
+
+        def unit_gain(unit):
+            j = unit % GROUPS
             gain[unit] = small.tile([P, 1], F32, name="gain")
-            nc.scalar.activation(out=gain[unit][:], in_=gamma_beta[:, j : j + 1], func=ACT.Copy, scale=inverse[:])
+            nc.scalar.activation(
+                out=gain[unit][:], in_=gamma_beta[:, j : j + 1], func=ACT.Copy, scale=inverse[unit][:]
+            )
+
+        def unit_shift(unit):
+            j = unit % GROUPS
             shift[unit] = small.tile([P, 1], F32, name="shift")
             nc.scalar.activation(
                 out=shift[unit][:],
@@ -207,14 +224,12 @@ def tile_spatialcgnl_pb_t_kernel(tc, y, Wz, gamma, beta, x, out):
                     op0=ALU.mult,
                     op1=ALU.add,
                 )
-                nc.gpsimd.tensor_scalar(
-                    out=half[:],
-                    in0=half[:],
-                    scalar1=1.0,
-                    scalar2=shift[unit][:],
-                    op0=ALU.mult,
-                    op1=ALU.add,
-                )
+                if unit < UNITS - 1:
+                    nc.gpsimd.tensor_scalar(
+                        out=half[:], in0=half[:], scalar1=1.0, scalar2=shift[unit][:], op0=ALU.mult, op1=ALU.add
+                    )
+                else:
+                    nc.scalar.activation(out=half[:], in_=half[:], func=ACT.Identity, bias=shift[unit][:], scale=1.0)
                 nc.sync.dma_start(out=out_rows[:, halves[h]], in_=half[:])
 
         def live(unit):
@@ -222,24 +237,38 @@ def tile_spatialcgnl_pb_t_kernel(tc, y, Wz, gamma, beta, x, out):
 
         prepare_weights()
         prepare_affine()
-        regroup(0, 0)
+        regroup_vector(0, 0)
+        regroup_scalar(0, 0, 0)
+        regroup_scalar(0, 0, 1)
         for step in range(UNITS + 3):
             entering, multiplied, measured, scaled = step, step - 1, step - 2, step - 3
             if live(multiplied):
                 quantise_and_multiply(multiplied, 1)
-            if live(measured):
-                unit_variance(measured)
             if live(scaled):
                 scale_add_shift_store(scaled)
                 if live(multiplied):
                     partition_moments(multiplied)
             if live(entering):
-                regroup(entering, 1)
-            if live(multiplied) and not live(scaled):
-                partition_moments(multiplied)
+                regroup_vector(entering, 1)
+                regroup_scalar(entering, 1, 0)
             if live(measured):
-                gain_and_shift(measured)
+                unit_variance(measured)
+            if live(entering):
+                regroup_scalar(entering, 1, 1)
+            if live(measured):
+                inverse_deviation(measured)
+            if live(multiplied):
+                if not live(scaled):
+                    partition_moments(multiplied)
+                unit_mean(multiplied)
             if live(entering):
                 quantise_and_multiply(entering, 0)
             if live(entering + 1):
-                regroup(entering + 1, 0)
+                regroup_vector(entering + 1, 0)
+                regroup_scalar(entering + 1, 0, 0)
+            if live(measured):
+                unit_gain(measured)
+            if live(entering + 1):
+                regroup_scalar(entering + 1, 0, 1)
+            if live(measured):
+                unit_shift(measured)

@@ -39,7 +39,7 @@ def tile_spatialcgnl_pb_t_kernel(tc, y, Wz, gamma, beta, x, out):
         inputs = stack.enter_context(tc.tile_pool(name="inputs", bufs=1))
         work = stack.enter_context(tc.tile_pool(name="work", bufs=3))
         small = stack.enter_context(tc.tile_pool(name="small", bufs=4))
-        results = stack.enter_context(tc.tile_pool(name="results", bufs=3))
+        results = stack.enter_context(tc.tile_pool(name="results", bufs=UNITS))
         z_psum = stack.enter_context(tc.psum_pool(name="z_psum", bufs=3 * HALVES))
         moment_psum = stack.enter_context(tc.psum_pool(name="moment_psum", bufs=2))
 

@@ -26,7 +26,7 @@ PASSES = CG // K_PASS
 BANK = 512
 HALVES = HW // BANK
 
-VECTOR_COLS = 368
+VECTOR_COLS = 400
 
 FLOPS = 2 * UNITS * CO * CG * HW
 
@@ -211,9 +211,8 @@ def tile_spatialcgnl_pb_t_kernel(tc, y, Wz, gamma, beta, x, out):
                 scale=gain[unit][:],
             )
 
-        def scale_add_shift_store(unit):
-            b, j = divmod(unit, GROUPS)
-            out_rows = out[b, j * CO : (j + 1) * CO].rearrange("o h w -> o (h w)")
+        def scale_and_add(unit):
+            result[unit] = []
             for h in range(HALVES):
                 half = results.tile([P, BANK], F32, name="result_%d" % h)
                 nc.vector.scalar_tensor_tensor(
@@ -224,13 +223,14 @@ def tile_spatialcgnl_pb_t_kernel(tc, y, Wz, gamma, beta, x, out):
                     op0=ALU.mult,
                     op1=ALU.add,
                 )
-                if unit < UNITS - 1:
-                    nc.gpsimd.tensor_scalar(
-                        out=half[:], in0=half[:], scalar1=1.0, scalar2=shift[unit][:], op0=ALU.mult, op1=ALU.add
-                    )
-                else:
-                    nc.scalar.activation(out=half[:], in_=half[:], func=ACT.Identity, bias=shift[unit][:], scale=1.0)
-                nc.sync.dma_start(out=out_rows[:, halves[h]], in_=half[:])
+                result[unit].append(half)
+
+        def shift_and_store(unit, h):
+            b, j = divmod(unit, GROUPS)
+            out_rows = out[b, j * CO : (j + 1) * CO].rearrange("o h w -> o (h w)")
+            half = result[unit][h]
+            nc.scalar.activation(out=half[:], in_=half[:], func=ACT.Identity, bias=shift[unit][:], scale=1.0)
+            nc.sync.dma_start(out=out_rows[:, halves[h]], in_=half[:])
 
         def live(unit):
             return 0 <= unit < UNITS
@@ -245,7 +245,7 @@ def tile_spatialcgnl_pb_t_kernel(tc, y, Wz, gamma, beta, x, out):
             if live(multiplied):
                 quantise_and_multiply(multiplied, 1)
             if live(scaled):
-                scale_add_shift_store(scaled)
+                scale_and_add(scaled)
                 if live(multiplied):
                     partition_moments(multiplied)
             if live(entering):
@@ -257,6 +257,8 @@ def tile_spatialcgnl_pb_t_kernel(tc, y, Wz, gamma, beta, x, out):
                 regroup_scalar(entering, 1, 1)
             if live(measured):
                 inverse_deviation(measured)
+            if live(scaled):
+                shift_and_store(scaled, 0)
             if live(multiplied):
                 if not live(scaled):
                     partition_moments(multiplied)
@@ -268,6 +270,8 @@ def tile_spatialcgnl_pb_t_kernel(tc, y, Wz, gamma, beta, x, out):
                 regroup_scalar(entering + 1, 0, 0)
             if live(measured):
                 unit_gain(measured)
+            if live(scaled):
+                shift_and_store(scaled, 1)
             if live(entering + 1):
                 regroup_scalar(entering + 1, 0, 1)
             if live(measured):

@@ -38,6 +38,7 @@ def tile_spatialcgnl_pb_t_kernel(tc, y, Wz, gamma, beta, x, out):
         consts = stack.enter_context(tc.tile_pool(name="consts", bufs=1))
         inputs = stack.enter_context(tc.tile_pool(name="inputs", bufs=1))
         work = stack.enter_context(tc.tile_pool(name="work", bufs=3))
+        regrouped = stack.enter_context(tc.tile_pool(name="regrouped", bufs=4))
         small = stack.enter_context(tc.tile_pool(name="small", bufs=4))
         results = stack.enter_context(tc.tile_pool(name="results", bufs=UNITS))
         z_psum = stack.enter_context(tc.psum_pool(name="z_psum", bufs=3 * HALVES))
@@ -60,15 +61,14 @@ def tile_spatialcgnl_pb_t_kernel(tc, y, Wz, gamma, beta, x, out):
             nc.sync.dma_start(out=x_raw[unit][:], in_=x[b, j * CO : (j + 1) * CO].rearrange("o h w -> o (h w)"))
 
         w_raw = consts.tile([P, GROUPS * CG], BF16)
-        nc.sync.dma_start(
-            out=w_raw[:].rearrange("o (j k) -> o j k", j=GROUPS), in_=Wz.rearrange("j o k -> o j k")
-        )
+        for j in range(GROUPS):
+            nc.sync.dma_start(out=w_raw[:, j * CG : (j + 1) * CG], in_=Wz[j])
+        load_y(0, 0)
+        load_y(0, 1)
         affine_rows = consts.tile([P, P], BF16)
         nc.vector.memset(affine_rows[:], 0.0)
         nc.sync.dma_start(out=affine_rows[0:GROUPS, :], in_=gamma.rearrange("(j o) -> j o", j=GROUPS))
         nc.sync.dma_start(out=affine_rows[GROUPS : 2 * GROUPS, :], in_=beta.rearrange("(j o) -> j o", j=GROUPS))
-        load_y(0, 0)
-        load_y(0, 1)
         for unit in range(1, UNITS):
             load_y(unit, 0)
             load_y(unit, 1)
@@ -100,11 +100,14 @@ def tile_spatialcgnl_pb_t_kernel(tc, y, Wz, gamma, beta, x, out):
                 nc.vector.tensor_copy(out=w_grouped_words[:, j], in_=w_t[:].rearrange("p c u o -> p c o u"))
             nc.vector.quantize_mx(out=w_codes[:].bitcast(FP8X4), scales=w_scales[:], in_=w_grouped[:])
 
-        def prepare_affine():
+        affine_t = z_psum.tile([P, P], F32, tag="z")
+
+        def transpose_affine():
             affine_rows_f32 = consts.tile([P, P], F32)
             nc.vector.tensor_copy(out=affine_rows_f32[:], in_=affine_rows[:])
-            affine_t = z_psum.tile([P, P], F32, tag="z")
             nc.tensor.transpose(affine_t[:], affine_rows_f32[:], identity[:])
+
+        def keep_affine():
             nc.vector.tensor_copy(out=gamma_beta[:], in_=affine_t[:, 0 : 2 * GROUPS])
 
         vector_cols = slice(0, VECTOR_COLS)
@@ -129,7 +132,7 @@ def tile_spatialcgnl_pb_t_kernel(tc, y, Wz, gamma, beta, x, out):
             return tile_ap[:, :, cols].rearrange("p t (n i) -> p n t i", i=4)
 
         def regroup_vector(unit, c):
-            grouped[unit, c] = work.tile([P, HW, PACK], BF16, name="grouped", align_bytes=64)
+            grouped[unit, c] = regrouped.tile([P, HW, PACK], BF16, name="grouped", align_bytes=64)
             nc.vector.tensor_copy(
                 out=interleaved(grouped[unit, c], vector_cols), in_=rows_of(y_raw[unit, c], vector_cols)
             )
@@ -232,11 +235,32 @@ def tile_spatialcgnl_pb_t_kernel(tc, y, Wz, gamma, beta, x, out):
             nc.scalar.activation(out=half[:], in_=half[:], func=ACT.Identity, bias=shift[unit][:], scale=1.0)
             nc.sync.dma_start(out=out_rows[:, halves[h]], in_=half[:])
 
+        def last_unit_out(unit):
+            b, j = divmod(unit, GROUPS)
+            out_rows = out[b, j * CO : (j + 1) * CO].rearrange("o h w -> o (h w)")
+            quarter = BANK // 2
+            for h in range(HALVES):
+                half = results.tile([P, BANK], F32, name="result_%d" % h)
+                for lo in (0, quarter):
+                    cols = slice(lo, lo + quarter)
+                    unit_cols = slice(h * BANK + lo, h * BANK + lo + quarter)
+                    nc.vector.scalar_tensor_tensor(
+                        out=half[:, cols],
+                        in0=z[unit][h][:, cols],
+                        scalar=gain[unit][:],
+                        in1=x_raw[unit][:, unit_cols],
+                        op0=ALU.mult,
+                        op1=ALU.add,
+                    )
+                    nc.scalar.activation(
+                        out=half[:, cols], in_=half[:, cols], func=ACT.Identity, bias=shift[unit][:], scale=1.0
+                    )
+                    nc.sync.dma_start(out=out_rows[:, unit_cols], in_=half[:, cols])
+
         def live(unit):
             return 0 <= unit < UNITS
 
         prepare_weights()
-        prepare_affine()
         regroup_vector(0, 0)
         regroup_scalar(0, 0, 0)
         regroup_scalar(0, 0, 1)
@@ -244,6 +268,9 @@ def tile_spatialcgnl_pb_t_kernel(tc, y, Wz, gamma, beta, x, out):
             entering, multiplied, measured, scaled = step, step - 1, step - 2, step - 3
             if live(multiplied):
                 quantise_and_multiply(multiplied, 1)
+            if scaled == UNITS - 1:
+                last_unit_out(scaled)
+                break
             if live(scaled):
                 scale_and_add(scaled)
                 if live(multiplied):
@@ -263,8 +290,12 @@ def tile_spatialcgnl_pb_t_kernel(tc, y, Wz, gamma, beta, x, out):
                 if not live(scaled):
                     partition_moments(multiplied)
                 unit_mean(multiplied)
+            if step == 0:
+                transpose_affine()
             if live(entering):
                 quantise_and_multiply(entering, 0)
+            if step == 0:
+                keep_affine()
             if live(entering + 1):
                 regroup_vector(entering + 1, 0)
                 regroup_scalar(entering + 1, 0, 0)

@@ -28,6 +28,8 @@ HALVES = HW // BANK
 
 VECTOR_COLS = 400
 
+RUN = 8
+
 FLOPS = 2 * UNITS * CO * CG * HW
 
 
@@ -126,10 +128,10 @@ def tile_spatialcgnl_pb_t_kernel(tc, y, Wz, gamma, beta, x, out):
         result = {}
 
         def interleaved(tile_ap, cols):
-            return tile_ap[:, cols, :].rearrange("p (n i) t -> p n t i", i=4)
+            return tile_ap[:, cols, :].rearrange("p (n i) t -> p n t i", i=RUN)
 
         def rows_of(tile_ap, cols):
-            return tile_ap[:, :, cols].rearrange("p t (n i) -> p n t i", i=4)
+            return tile_ap[:, :, cols].rearrange("p t (n i) -> p n t i", i=RUN)
 
         def regroup_vector(unit, c):
             grouped[unit, c] = regrouped.tile([P, HW, PACK], BF16, name="grouped", align_bytes=64)

@@ -275,8 +275,6 @@ def tile_spatialcgnl_pb_t_kernel(tc, y, Wz, gamma, beta, x, out):
                 break
             if live(scaled):
                 scale_and_add(scaled)
-                if live(multiplied):
-                    partition_moments(multiplied)
             if live(entering):
                 regroup_vector(entering, 1)
                 regroup_scalar(entering, 1, 0)
@@ -289,13 +287,13 @@ def tile_spatialcgnl_pb_t_kernel(tc, y, Wz, gamma, beta, x, out):
             if live(scaled):
                 shift_and_store(scaled, 0)
             if live(multiplied):
-                if not live(scaled):
-                    partition_moments(multiplied)
-                unit_mean(multiplied)
+                partition_moments(multiplied)
             if step == 0:
                 transpose_affine()
             if live(entering):
                 quantise_and_multiply(entering, 0)
+            if live(multiplied):
+                unit_mean(multiplied)
             if step == 0:
                 keep_affine()
             if live(entering + 1):

@@ -49,13 +49,14 @@ def tile_spatialcgnl_pb_t_kernel(tc, y, Wz, gamma, beta, x, out):
         y_raw = {}
         x_raw = {}
 
-        def load_y(unit, c):
+        def load_y(unit, c, column_ranges=(slice(0, HW),)):
             b, j = divmod(unit, GROUPS)
             y_raw[unit, c] = inputs.tile([P, PACK, HW], BF16, name="y_raw_%d_%d" % (unit, c))
-            nc.sync.dma_start(
-                out=y_raw[unit, c][:],
-                in_=y[b, j, c * K_PASS : (c + 1) * K_PASS, :].rearrange("(p t) n -> p t n", t=PACK),
-            )
+            for cols in column_ranges:
+                nc.sync.dma_start(
+                    out=y_raw[unit, c][:, :, cols],
+                    in_=y[b, j, c * K_PASS : (c + 1) * K_PASS, cols].rearrange("(p t) n -> p t n", t=PACK),
+                )
 
         def load_x(unit):
             b, j = divmod(unit, GROUPS)
@@ -65,7 +66,7 @@ def tile_spatialcgnl_pb_t_kernel(tc, y, Wz, gamma, beta, x, out):
         w_raw = consts.tile([P, GROUPS * CG], BF16)
         for j in range(GROUPS):
             nc.sync.dma_start(out=w_raw[:, j * CG : (j + 1) * CG], in_=Wz[j])
-        load_y(0, 0)
+        load_y(0, 0, (slice(VECTOR_COLS, HW), slice(0, VECTOR_COLS)))
         load_y(0, 1)
         affine_rows = consts.tile([P, P], BF16)
         nc.vector.memset(affine_rows[:], 0.0)
@@ -275,6 +276,19 @@ def tile_spatialcgnl_pb_t_kernel(tc, y, Wz, gamma, beta, x, out):
                 break
             if live(scaled):
                 scale_and_add(scaled)
+            if not live(entering):
+                if live(measured):
+                    unit_variance(measured)
+                if live(multiplied):
+                    partition_moments(multiplied)
+                    unit_mean(multiplied)
+                shift_and_store(scaled, 0)
+                if live(measured):
+                    inverse_deviation(measured)
+                    unit_gain(measured)
+                    unit_shift(measured)
+                shift_and_store(scaled, 1)
+                continue
             if live(entering):
                 regroup_vector(entering, 1)
                 regroup_scalar(entering, 1, 0)
@@ -282,8 +296,6 @@ def tile_spatialcgnl_pb_t_kernel(tc, y, Wz, gamma, beta, x, out):
                 unit_variance(measured)
             if live(entering):
                 regroup_scalar(entering, 1, 1)
-            if live(measured):
-                inverse_deviation(measured)
             if live(scaled):
                 shift_and_store(scaled, 0)
             if live(multiplied):
@@ -300,9 +312,11 @@ def tile_spatialcgnl_pb_t_kernel(tc, y, Wz, gamma, beta, x, out):
                 regroup_vector(entering + 1, 0)
                 regroup_scalar(entering + 1, 0, 0)
             if live(measured):
-                unit_gain(measured)
+                inverse_deviation(measured)
             if live(scaled):
                 shift_and_store(scaled, 1)
+            if live(measured):
+                unit_gain(measured)
             if live(entering + 1):
                 regroup_scalar(entering + 1, 0, 1)
             if live(measured):

from contextlib import ExitStack

import concourse.mybir as mybir
from concourse.masks import make_identity

F32 = mybir.dt.float32
BF16 = mybir.dt.bfloat16
U32 = mybir.dt.uint32
U8 = mybir.dt.uint8
FP8X4 = mybir.dt.float8_e4m3fn_x4
ALU = mybir.AluOpType
ACT = mybir.ActivationFunctionType

IMAGES = 4
GROUPS = 2
UNITS = IMAGES * GROUPS
CG = 1024
CO = 128
HW = 1024
EPS = 1e-5

P = 128
PACK = 4
K_PASS = P * PACK
PASSES = CG // K_PASS
BANK = 512
HALVES = HW // BANK

VECTOR_COLS = 400

RUN = 8

FLOPS = 2 * UNITS * CO * CG * HW


def tile_spatialcgnl_pb_t_kernel(tc, y, Wz, gamma, beta, x, out):
    nc = tc.nc
    with ExitStack() as stack:
        stack.enter_context(tc.manual_schedule())
        consts = stack.enter_context(tc.tile_pool(name="consts", bufs=1))
        inputs = stack.enter_context(tc.tile_pool(name="inputs", bufs=1))
        work = stack.enter_context(tc.tile_pool(name="work", bufs=3))
        regrouped = stack.enter_context(tc.tile_pool(name="regrouped", bufs=4))
        small = stack.enter_context(tc.tile_pool(name="small", bufs=4))
        results = stack.enter_context(tc.tile_pool(name="results", bufs=UNITS))
        z_psum = stack.enter_context(tc.psum_pool(name="z_psum", bufs=3 * HALVES))
        moment_psum = stack.enter_context(tc.psum_pool(name="moment_psum", bufs=2))

        y_raw = {}
        x_raw = {}

        def load_y(unit, c, column_ranges=(slice(0, HW),)):
            b, j = divmod(unit, GROUPS)
            y_raw[unit, c] = inputs.tile([P, PACK, HW], BF16, name="y_raw_%d_%d" % (unit, c))
            for cols in column_ranges:
                nc.sync.dma_start(
                    out=y_raw[unit, c][:, :, cols],
                    in_=y[b, j, c * K_PASS : (c + 1) * K_PASS, cols].rearrange("(p t) n -> p t n", t=PACK),
                )

        def load_x(unit):
            b, j = divmod(unit, GROUPS)
            x_raw[unit] = inputs.tile([P, HW], BF16, name="x_raw_%d" % unit)
            nc.sync.dma_start(out=x_raw[unit][:], in_=x[b, j * CO : (j + 1) * CO].rearrange("o h w -> o (h w)"))

        w_raw = consts.tile([P, GROUPS * CG], BF16)
        for j in range(GROUPS):
            nc.sync.dma_start(out=w_raw[:, j * CG : (j + 1) * CG], in_=Wz[j])
        load_y(0, 0, (slice(VECTOR_COLS, HW), slice(0, VECTOR_COLS)))
        load_y(0, 1)
        affine_rows = consts.tile([P, P], BF16)
        nc.vector.memset(affine_rows[:], 0.0)
        nc.sync.dma_start(out=affine_rows[0:GROUPS, :], in_=gamma.rearrange("(j o) -> j o", j=GROUPS))
        nc.sync.dma_start(out=affine_rows[GROUPS : 2 * GROUPS, :], in_=beta.rearrange("(j o) -> j o", j=GROUPS))
        for unit in range(1, UNITS):
            load_y(unit, 0)
            load_y(unit, 1)
            load_x(unit - 1)
        load_x(UNITS - 1)

        identity = consts.tile([P, P], F32)
        make_identity(nc, identity[:])
        minus_average = consts.tile([P, P], F32)
        nc.vector.memset(minus_average[:], -1.0 / P)
        eps = consts.tile([P, 1], F32)
        nc.vector.memset(eps[:], EPS)
        table_warmer = consts.tile([P, 1], F32)
        nc.scalar.activation(out=table_warmer[:], in_=eps[:], func=ACT.Abs_reciprocal_sqrt)

        w_codes = consts.tile([P, GROUPS * PASSES * CO], U32, align_bytes=64)
        w_scales = consts.tile([P, GROUPS * PASSES * CO], U8, align_bytes=64)
        gamma_beta = consts.tile([P, 2 * GROUPS], F32)

        def prepare_weights():
            w_words = w_raw[:].bitcast(F32).rearrange("o (j c p u) -> o j c u p", j=GROUPS, c=PASSES, u=2)
            w_grouped = consts.tile([P, GROUPS * PASSES * CO * PACK], BF16, align_bytes=64)
            w_grouped_words = w_grouped[:].bitcast(F32).rearrange("p (j c o u) -> p j c o u", j=GROUPS, c=PASSES, u=2)
            for j in range(GROUPS):
                w_t = z_psum.tile([P, PASSES, 2, CO], F32, tag="z")
                for c in range(PASSES):
                    for u in range(2):
                        nc.tensor.transpose(w_t[:, c, u, :], w_words[:, j, c, u, :], identity[:])
                nc.vector.tensor_copy(out=w_grouped_words[:, j], in_=w_t[:].rearrange("p c u o -> p c o u"))
            nc.vector.quantize_mx(out=w_codes[:].bitcast(FP8X4), scales=w_scales[:], in_=w_grouped[:])

        affine_t = z_psum.tile([P, P], F32, tag="z")

        def transpose_affine():
            affine_rows_f32 = consts.tile([P, P], F32)
            nc.vector.tensor_copy(out=affine_rows_f32[:], in_=affine_rows[:])
            nc.tensor.transpose(affine_t[:], affine_rows_f32[:], identity[:])

        def keep_affine():
            nc.vector.tensor_copy(out=gamma_beta[:], in_=affine_t[:, 0 : 2 * GROUPS])

        vector_cols = slice(0, VECTOR_COLS)
        scalar_middle = (VECTOR_COLS + HW) // 2
        scalar_parts = [slice(VECTOR_COLS, scalar_middle), slice(scalar_middle, HW)]
        halves = [slice(h * BANK, (h + 1) * BANK) for h in range(HALVES)]

        grouped = {}
        z = {}
        bank_stats = {}
        mean_var = {}
        inverse = {}
        moments = {}
        gain = {}
        shift = {}
        result = {}

        def interleaved(tile_ap, cols):
            return tile_ap[:, cols, :].rearrange("p (n i) t -> p n t i", i=RUN)

        def rows_of(tile_ap, cols):
            return tile_ap[:, :, cols].rearrange("p t (n i) -> p n t i", i=RUN)

        def regroup_vector(unit, c):
            grouped[unit, c] = regrouped.tile([P, HW, PACK], BF16, name="grouped", align_bytes=64)
            nc.vector.tensor_copy(
                out=interleaved(grouped[unit, c], vector_cols), in_=rows_of(y_raw[unit, c], vector_cols)
            )

        def regroup_scalar(unit, c, part):
            nc.scalar.copy(
                out=interleaved(grouped[unit, c], scalar_parts[part]), in_=rows_of(y_raw[unit, c], scalar_parts[part])
            )

        def quantise_and_multiply(unit, c):
            j = unit % GROUPS
            y_codes = work.tile([P, HW], U32, align_bytes=64)
            y_scales = work.tile([P, HW], U8, align_bytes=64)
            nc.vector.quantize_mx(
                out=y_codes[:].bitcast(FP8X4),
                scales=y_scales[:],
                in_=grouped[unit, c][:].rearrange("p n t -> p (n t)"),
            )
            if c == 0:
                z[unit] = [z_psum.tile([P, BANK], F32, name="z_%d" % h, tag="z") for h in range(HALVES)]
            w_cols = slice((j * PASSES + c) * CO, (j * PASSES + c + 1) * CO)
            for h in range(HALVES):
                nc.tensor.matmul_mx(
                    out=z[unit][h][:],
                    lhsT=w_codes[:, w_cols].bitcast(FP8X4),
                    lhsT_scale=w_scales[:, w_cols],
                    rhs=y_codes[:, halves[h]].bitcast(FP8X4),
                    rhs_scale=y_scales[:, halves[h]],
                    start=(c == 0),
                    stop=(c == PASSES - 1),
                )

        def partition_moments(unit):
            bank_stats[unit] = small.tile([P, HALVES, 6], F32, name="bank_stats")
            for h in range(HALVES):
                nc.vector.bn_stats(out=bank_stats[unit][:, h, :], in_=z[unit][h][:])

        def unit_mean(unit):
            mean_var[unit] = small.tile([P, 2], F32, name="mean_var")
            nc.vector.bn_aggr(out=mean_var[unit][:], in_=bank_stats[unit][:].rearrange("p h s -> p (h s)"))
            moments[unit] = moment_psum.tile([P, 2], F32, name="moments")
            nc.tensor.matmul(
                out=moments[unit][:, 0:1], lhsT=minus_average[:], rhs=mean_var[unit][:, 0:1], start=True, stop=True
            )

        def unit_variance(unit):
            centred_sq = small.tile([P, 1], F32)
            nc.scalar.activation(
                out=centred_sq[:], in_=moments[unit][:, 0:1], func=ACT.Square, bias=mean_var[unit][:, 0:1], scale=1.0
            )
            nc.tensor.matmul(
                out=moments[unit][:, 1:2], lhsT=minus_average[:], rhs=mean_var[unit][:, 1:2], start=True, stop=False
            )
            nc.tensor.matmul(
                out=moments[unit][:, 1:2], lhsT=minus_average[:], rhs=centred_sq[:], start=False, stop=True
            )

        def inverse_deviation(unit):
            inverse[unit] = small.tile([P, 1], F32, name="inverse")
            nc.scalar.activation(
                out=inverse[unit][:], in_=moments[unit][:, 1:2], func=ACT.Abs_reciprocal_sqrt, bias=eps[:], scale=-1.0
            )

        def unit_gain(unit):
            j = unit % GROUPS
            gain[unit] = small.tile([P, 1], F32, name="gain")
            nc.scalar.activation(
                out=gain[unit][:], in_=gamma_beta[:, j : j + 1], func=ACT.Copy, scale=inverse[unit][:]
            )

        def unit_shift(unit):
            j = unit % GROUPS
            shift[unit] = small.tile([P, 1], F32, name="shift")
            nc.scalar.activation(
                out=shift[unit][:],
                in_=moments[unit][:, 0:1],
                func=ACT.Identity,
                bias=gamma_beta[:, GROUPS + j : GROUPS + j + 1],
                scale=gain[unit][:],
            )

        def scale_and_add(unit):
            result[unit] = []
            for h in range(HALVES):
                half = results.tile([P, BANK], F32, name="result_%d" % h)
                nc.vector.scalar_tensor_tensor(
                    out=half[:],
                    in0=z[unit][h][:],
                    scalar=gain[unit][:],
                    in1=x_raw[unit][:, halves[h]],
                    op0=ALU.mult,
                    op1=ALU.add,
                )
                result[unit].append(half)

        def shift_and_store(unit, h):
            b, j = divmod(unit, GROUPS)
            out_rows = out[b, j * CO : (j + 1) * CO].rearrange("o h w -> o (h w)")
            half = result[unit][h]
            nc.scalar.activation(out=half[:], in_=half[:], func=ACT.Identity, bias=shift[unit][:], scale=1.0)
            nc.sync.dma_start(out=out_rows[:, halves[h]], in_=half[:])

        def last_unit_out(unit):
            b, j = divmod(unit, GROUPS)
            out_rows = out[b, j * CO : (j + 1) * CO].rearrange("o h w -> o (h w)")
            quarter = BANK // 2
            for h in range(HALVES):
                half = results.tile([P, BANK], F32, name="result_%d" % h)
                for lo in (0, quarter):
                    cols = slice(lo, lo + quarter)
                    unit_cols = slice(h * BANK + lo, h * BANK + lo + quarter)
                    nc.vector.scalar_tensor_tensor(
                        out=half[:, cols],
                        in0=z[unit][h][:, cols],
                        scalar=gain[unit][:],
                        in1=x_raw[unit][:, unit_cols],
                        op0=ALU.mult,
                        op1=ALU.add,
                    )
                    nc.scalar.activation(
                        out=half[:, cols], in_=half[:, cols], func=ACT.Identity, bias=shift[unit][:], scale=1.0
                    )
                    nc.sync.dma_start(out=out_rows[:, unit_cols], in_=half[:, cols])

        def live(unit):
            return 0 <= unit < UNITS

        prepare_weights()
        regroup_vector(0, 0)
        regroup_scalar(0, 0, 0)
        regroup_scalar(0, 0, 1)
        for step in range(UNITS + 3):
            entering, multiplied, measured, scaled = step, step - 1, step - 2, step - 3
            if live(multiplied):
                quantise_and_multiply(multiplied, 1)
            if scaled == UNITS - 1:
                last_unit_out(scaled)
                break
            if live(scaled):
                scale_and_add(scaled)
            if not live(entering):
                if live(measured):
                    unit_variance(measured)
                if live(multiplied):
                    partition_moments(multiplied)
                    unit_mean(multiplied)
                shift_and_store(scaled, 0)
                if live(measured):
                    inverse_deviation(measured)
                    unit_gain(measured)
                    unit_shift(measured)
                shift_and_store(scaled, 1)
                continue
            if live(entering):
                regroup_vector(entering, 1)
                regroup_scalar(entering, 1, 0)
            if live(measured):
                unit_variance(measured)
            if live(entering):
                regroup_scalar(entering, 1, 1)
            if live(scaled):
                shift_and_store(scaled, 0)
            if live(multiplied):
                partition_moments(multiplied)
            if step == 0:
                transpose_affine()
            if live(entering):
                quantise_and_multiply(entering, 0)
            if live(multiplied):
                unit_mean(multiplied)
            if step == 0:
                keep_affine()
            if live(entering + 1):
                regroup_vector(entering + 1, 0)
                regroup_scalar(entering + 1, 0, 0)
            if live(measured):
                inverse_deviation(measured)
            if live(scaled):
                shift_and_store(scaled, 1)
            if live(measured):
                unit_gain(measured)
            if live(entering + 1):
                regroup_scalar(entering + 1, 0, 1)
            if live(measured):
                unit_shift(measured)
